import numpy as np
import ml_dtypes


def mxq(x, axis, fmt="e4m3"):
    dtype, down = {"e4m3": (ml_dtypes.float8_e4m3fn, 7), "e5m2": (ml_dtypes.float8_e5m2, 14)}[fmt]
    v = np.moveaxis(np.asarray(x, np.float32).astype(ml_dtypes.bfloat16).astype(np.float64), axis, -1)
    blocks = v.reshape(v.shape[:-1] + (-1, 32))
    amax = np.abs(blocks).max(-1, keepdims=True)
    byte = np.maximum(np.where(amax > 0, np.frexp(amax)[1] - 1 + 127, 0) - down, 1)
    scale = np.exp2(byte - 127.0)
    codes = (blocks / scale).astype(np.float32).astype(dtype).astype(np.float64)
    return np.moveaxis((codes * scale).reshape(v.shape), -1, axis)


WIDE = False


def mx_kscale(k):
    if not WIDE:
        return np.ones(k)
    levels = np.array([10, -10, 5, -5, 0])
    a = np.random.permutation(np.resize(levels, k // 512 * 4)).reshape(k // 512, 4)
    idx = np.arange(k)
    return np.exp2(a[idx // 512, idx % 128 // 32])


BF16 = ml_dtypes.bfloat16


def bf(x):
    return np.asarray(x, np.float32).astype(BF16)


def f64(x):
    return np.asarray(x).astype(np.float64)


E2M1 = np.array([0.0, 0.5, 1.0, 1.5, 2.0, 3.0, 4.0, 6.0, -0.0, -0.5, -1.0, -1.5, -2.0, -3.0, -4.0, -6.0])


def pack_weight(w, fmt):
    k, n = w.shape
    w = f64(bf(w)).reshape(k // 32, 32, n)
    amax = np.abs(w).max(1)
    if fmt == "e4m3":
        byte = np.frexp(amax)[1] - 1 + 127 - 7
    else:
        mant, ex = np.frexp(amax / 6.0)
        byte = np.where(mant > 0.5, ex, ex - 1) + 127
    byte = np.clip(np.where(amax > 0, byte, 1), 1, 254)
    scaled = (w * np.exp2(127.0 - byte)[:, None, :]).reshape(k, n).astype(np.float32)
    by_word = np.ascontiguousarray(scaled.reshape(k // 512, 128, 4, n).transpose(0, 1, 3, 2))
    if fmt == "e4m3":
        words = by_word.astype(ml_dtypes.float8_e4m3fn).view(np.uint8)
    else:
        c = by_word.astype(ml_dtypes.float4_e2m1fn).view(np.uint8) & 0xF
        words = c[..., 0::2] | (c[..., 1::2] << 4)
    return np.ascontiguousarray(words), np.ascontiguousarray(byte.astype(np.uint8).reshape(k // 512, 16, n))


def unpack_weight(words, scales, fmt):
    g, p, n, _ = words.shape
    if fmt == "e4m3":
        vals = np.ascontiguousarray(words).view(ml_dtypes.float8_e4m3fn).astype(np.float64)
    else:
        nib = np.empty((g, p, n, 4), np.uint8)
        nib[..., 0::2] = words & 0xF
        nib[..., 1::2] = words >> 4
        vals = E2M1[nib]
    vals = vals * np.repeat(np.exp2(scales.astype(np.float64) - 127.0), 8, axis=1)[..., None]
    return vals.transpose(0, 1, 3, 2).reshape(g * 512, n)

def pack4(w):
    words, scales = pack_weight(w, "e2m1")
    return words.reshape(words.shape[0], 128, -1), scales


def unpack4(words, scales):
    return unpack_weight(words.reshape(words.shape[0], 128, -1, 2), scales, "e2m1")


B, C, H, W, RQ, RV = 1, 8192, 16, 8, 8, 2
DQ, DV = C // RQ, C // RV
N = H * W


def maxpool2(x):
    b, c, h, w = x.shape
    return x.reshape(b, c, h // 2, 2, w // 2, 2).max(axis=(3, 5))


def setup_inputs():
    s = mx_kscale(C)
    imgs = bf(np.random.standard_normal((B, C, H, W)) * s[None, :, None, None])
    w_kv = np.random.standard_normal((DQ + DV, C)) * 0.5 / np.sqrt(C) / s[None, :]
    words, scales = pack4(np.ascontiguousarray(w_kv.T))
    return {"imgs": imgs, "w_kv_words": words, "w_kv_scales": scales}


def reference(imgs, w_kv_words, w_kv_scales):
    x = f64(imgs).reshape(B, C, N)
    kv = (unpack4(w_kv_words, w_kv_scales).T @ mxq(x, 1, "e4m3")).reshape(B, DQ + DV, H, W)
    return maxpool2(kv[:, :DQ]), maxpool2(kv[:, DQ:])

@@ -1,0 +1,138 @@
+from contextlib import ExitStack
+
+import concourse.mybir as mybir
+from concourse.masks import make_identity
+
+F32 = mybir.dt.float32
+BF16 = mybir.dt.bfloat16
+I32 = mybir.dt.int32
+U32 = mybir.dt.uint32
+U8 = mybir.dt.uint8
+FP8X4 = mybir.dt.float8_e4m3fn_x4
+FP4X4 = mybir.dt.float4_e2m1fn_x4
+
+P = 128
+PACK = 4
+CHANNELS = 8192
+PASSES = CHANNELS // (P * PACK)
+PIXELS = 128
+WINDOWS = 32
+WINDOW = 4
+KEY_ROWS = 1024
+VALUE_ROWS = 4096
+OUT_ROWS = KEY_ROWS + VALUE_ROWS
+BANK = 512
+PSUM_BANKS = 8
+BLOCKS = BANK // P
+
+QUANT_PASSES = 4
+LOAD_BYTES = 8192
+SCALE_LOAD_BYTES = 16384
+WORD_BUFS = 10
+
+FLOPS = 2 * OUT_ROWS * CHANNELS * PIXELS
+
+
+def quantise_image(nc, keep, imgs, img_codes, img_scales):
+    raw = keep.tile([P, PASSES, PACK, PIXELS], BF16)
+    grouped = keep.tile([P, PASSES, PIXELS, PACK], BF16, align_bytes=64)
+    by_pass = imgs.rearrange("(g p t) h w -> p g t (h w)", p=P, t=PACK)
+    chunk_starts = range(0, PASSES, QUANT_PASSES)
+    for g in chunk_starts:
+        nc.sync.dma_start(out=raw[:, g : g + QUANT_PASSES], in_=by_pass[:, g : g + QUANT_PASSES])
+    for g in chunk_starts:
+        nc.vector.tensor_copy(
+            out=grouped[:, g : g + QUANT_PASSES],
+            in_=raw[:, g : g + QUANT_PASSES].rearrange("p g t x -> p g x t"),
+        )
+    for g in chunk_starts:
+        columns = slice(g * PIXELS, (g + QUANT_PASSES) * PIXELS)
+        nc.vector.quantize_mx(
+            out=img_codes[:, columns].bitcast(FP8X4),
+            scales=img_scales[:, columns],
+            in_=grouped[:, g : g + QUANT_PASSES].rearrange("p g x t -> p (g x t)"),
+        )
+
+
+def load_scale_rows(nc, planes, scales_i32, first_row, rows):
+    passes_per_dma = SCALE_LOAD_BYTES // rows
+    for g in range(0, PASSES, passes_per_dma):
+        some = slice(g, g + passes_per_dma)
+        for q in range(8):
+            nc.sync.dma_start(
+                out=planes[32 * (q // 4) + q % 4 : P : 64, some, first_row : first_row + rows].bitcast(I32),
+                in_=scales_i32[some, q : 16 : 8, first_row // 4 : (first_row + rows) // 4].rearrange(
+                    "g q n -> q g n"
+                ),
+            )
+
+
+def tile_selfattentionconv2d_pa_k_kernel(tc, imgs, w_kv_words, w_kv_scales, out_0, out_1):
+    nc = tc.nc
+    words_i32 = w_kv_words.bitcast(I32)
+    scales_i32 = w_kv_scales.bitcast(I32)
+
+    with ExitStack() as ctx:
+        ctx.enter_context(tc.manual_schedule())
+        keep = ctx.enter_context(tc.tile_pool(name="keep", bufs=1))
+        stream = ctx.enter_context(tc.tile_pool(name="stream", bufs=WORD_BUFS))
+        drain = ctx.enter_context(tc.tile_pool(name="drain", bufs=3))
+        psum = ctx.enter_context(tc.psum_pool(name="psum", bufs=PSUM_BANKS))
+
+        planes = keep.tile([P, PASSES, OUT_ROWS], U8, align_bytes=64)
+        for g in range(0, PASSES, QUANT_PASSES):
+            nc.vector.memset(planes[:, g : g + QUANT_PASSES, :].bitcast(I32), 0)
+
+        img_codes = keep.tile([P, PASSES * PIXELS], U32, align_bytes=64)
+        img_scales = keep.tile([P, PASSES * PIXELS], U8, align_bytes=64)
+        quantise_image(nc, keep, imgs[0], img_codes, img_scales)
+
+        identity = keep.tile([P, P], F32)
+        make_identity(nc, identity[:])
+        by_window = keep.tile([P, P], F32)
+        nc.vector.tensor_copy(
+            out=by_window[:].rearrange("p (i j a b) -> p i j a b", i=8, j=4, a=2, b=2),
+            in_=identity[:].rearrange("p (i a j b) -> p i j a b", i=8, a=2, j=4, b=2),
+        )
+
+        for first_row, rows, out in ((KEY_ROWS, VALUE_ROWS, out_1), (0, KEY_ROWS, out_0)):
+            load_scale_rows(nc, planes, scales_i32, first_row, rows)
+
+            banks = rows // BANK
+            sums = [psum.tile([P, BANK], F32, name="sums%d" % j, tag="bank") for j in range(banks)]
+            passes_per_load = LOAD_BYTES // (2 * rows)
+            for g0 in range(0, PASSES, passes_per_load):
+                words = stream.tile([P, passes_per_load, 2 * rows], U8, align_bytes=64, tag="words")
+                nc.sync.dma_start(
+                    out=words[:].bitcast(I32),
+                    in_=words_i32[g0 : g0 + passes_per_load, :, first_row // 2 : (first_row + rows) // 2].rearrange(
+                        "g p n -> p g n"
+                    ),
+                )
+                for g in range(g0, g0 + passes_per_load):
+                    for j in range(banks):
+                        nc.tensor.matmul_mx(
+                            out=sums[j][:],
+                            lhsT=img_codes[:, g * PIXELS : (g + 1) * PIXELS].bitcast(FP8X4),
+                            lhsT_scale=img_scales[:, g * PIXELS : (g + 1) * PIXELS],
+                            rhs=words[:, g - g0, 2 * BANK * j : 2 * BANK * (j + 1)].bitcast(FP4X4),
+                            rhs_scale=planes[:, g, first_row + BANK * j : first_row + BANK * (j + 1)],
+                            start=(g == 0),
+                            stop=(g == PASSES - 1),
+                        )
+
+            pooled = keep.tile([P, rows // P, WINDOWS], F32, name="pooled%d" % first_row)
+            for j in range(banks):
+                by_pixel = drain.tile([P, BANK], F32)
+                nc.scalar.copy(out=by_pixel[:], in_=sums[j][:])
+                by_row = psum.tile([P, BANK], F32, tag="bank")
+                for m in range(BLOCKS):
+                    block = slice(P * m, P * (m + 1))
+                    nc.tensor.transpose(by_row[:, block], by_pixel[:, block], by_window[:])
+                nc.vector.tensor_reduce(
+                    out=pooled[:, BLOCKS * j : BLOCKS * (j + 1), :],
+                    in_=by_row[:].rearrange("p (m w d) -> p m w d", m=BLOCKS, d=WINDOW),
+                    axis=mybir.AxisListType.X,
+                    op=mybir.AluOpType.max,
+                )
+            nc.scalar.dma_start(out=out[0].rearrange("(m p) i j -> p m (i j)", p=P), in_=pooled[:])

@@ -26,8 +26,7 @@ PSUM_BANKS = 8
 BLOCKS = BANK // P
 
 QUANT_PASSES = 4
-LOAD_BYTES = 8192
-SCALE_LOAD_BYTES = 16384
+SCALE_DMA_BYTES = 16384
 WORD_BUFS = 10
 
 FLOPS = 2 * OUT_ROWS * CHANNELS * PIXELS
@@ -54,9 +53,9 @@ def quantise_image(nc, keep, imgs, img_codes, img_scales):
         )
 
 
-def load_scale_rows(nc, planes, scales_i32, first_row, rows):
-    passes_per_dma = SCALE_LOAD_BYTES // rows
-    for g in range(0, PASSES, passes_per_dma):
+def load_scale_rows(nc, planes, scales_i32, first_pass, stretch, first_row, rows):
+    passes_per_dma = SCALE_DMA_BYTES // rows
+    for g in range(first_pass, first_pass + stretch, passes_per_dma):
         some = slice(g, g + passes_per_dma)
         for q in range(8):
             nc.sync.dma_start(
@@ -76,16 +75,17 @@ def tile_selfattentionconv2d_pa_k_kernel(tc, imgs, w_kv_words, w_kv_scales, out_
         ctx.enter_context(tc.manual_schedule())
         keep = ctx.enter_context(tc.tile_pool(name="keep", bufs=1))
         stream = ctx.enter_context(tc.tile_pool(name="stream", bufs=WORD_BUFS))
-        drain = ctx.enter_context(tc.tile_pool(name="drain", bufs=3))
+        drain = ctx.enter_context(tc.tile_pool(name="drain", bufs=PSUM_BANKS))
         psum = ctx.enter_context(tc.psum_pool(name="psum", bufs=PSUM_BANKS))
 
         planes = keep.tile([P, PASSES, OUT_ROWS], U8, align_bytes=64)
-        for g in range(0, PASSES, QUANT_PASSES):
-            nc.vector.memset(planes[:, g : g + QUANT_PASSES, :].bitcast(I32), 0)
+        nc.vector.memset(planes[:, 0 : PASSES // 2, :].bitcast(I32), 0)
 
         img_codes = keep.tile([P, PASSES * PIXELS], U32, align_bytes=64)
         img_scales = keep.tile([P, PASSES * PIXELS], U8, align_bytes=64)
         quantise_image(nc, keep, imgs[0], img_codes, img_scales)
+
+        nc.vector.memset(planes[:, PASSES // 2 : PASSES, :].bitcast(I32), 0)
 
         identity = keep.tile([P, P], F32)
         make_identity(nc, identity[:])
@@ -95,43 +95,48 @@ def tile_selfattentionconv2d_pa_k_kernel(tc, imgs, w_kv_words, w_kv_scales, out_
             in_=identity[:].rearrange("p (i a j b) -> p i j a b", i=8, a=2, j=4, b=2),
         )
 
-        for first_row, rows, out in ((KEY_ROWS, VALUE_ROWS, out_1), (0, KEY_ROWS, out_0)):
-            load_scale_rows(nc, planes, scales_i32, first_row, rows)
-
+        rounds = ((KEY_ROWS, VALUE_ROWS, PASSES // 2, 1, out_1), (0, KEY_ROWS, PASSES, 2, out_0))
+        for first_row, rows, stretch, passes_per_load, out in rounds:
             banks = rows // BANK
             sums = [psum.tile([P, BANK], F32, name="sums%d" % j, tag="bank") for j in range(banks)]
-            passes_per_load = LOAD_BYTES // (2 * rows)
-            for g0 in range(0, PASSES, passes_per_load):
-                words = stream.tile([P, passes_per_load, 2 * rows], U8, align_bytes=64, tag="words")
-                nc.sync.dma_start(
-                    out=words[:].bitcast(I32),
-                    in_=words_i32[g0 : g0 + passes_per_load, :, first_row // 2 : (first_row + rows) // 2].rearrange(
-                        "g p n -> p g n"
-                    ),
-                )
-                for g in range(g0, g0 + passes_per_load):
-                    for j in range(banks):
-                        nc.tensor.matmul_mx(
-                            out=sums[j][:],
-                            lhsT=img_codes[:, g * PIXELS : (g + 1) * PIXELS].bitcast(FP8X4),
-                            lhsT_scale=img_scales[:, g * PIXELS : (g + 1) * PIXELS],
-                            rhs=words[:, g - g0, 2 * BANK * j : 2 * BANK * (j + 1)].bitcast(FP4X4),
-                            rhs_scale=planes[:, g, first_row + BANK * j : first_row + BANK * (j + 1)],
-                            start=(g == 0),
-                            stop=(g == PASSES - 1),
-                        )
+            for first_pass in range(0, PASSES, stretch):
+                load_scale_rows(nc, planes, scales_i32, first_pass, stretch, first_row, rows)
+                for g0 in range(first_pass, first_pass + stretch, passes_per_load):
+                    words = stream.tile([P, passes_per_load, 2 * rows], U8, align_bytes=64, tag="words")
+                    nc.sync.dma_start(
+                        out=words[:].bitcast(I32),
+                        in_=words_i32[g0 : g0 + passes_per_load, :, first_row // 2 : (first_row + rows) // 2].rearrange(
+                            "g p n -> p g n"
+                        ),
+                    )
+                    for g in range(g0, g0 + passes_per_load):
+                        for j in range(banks):
+                            nc.tensor.matmul_mx(
+                                out=sums[j][:],
+                                lhsT=img_codes[:, g * PIXELS : (g + 1) * PIXELS].bitcast(FP8X4),
+                                lhsT_scale=img_scales[:, g * PIXELS : (g + 1) * PIXELS],
+                                rhs=words[:, g - g0, 2 * BANK * j : 2 * BANK * (j + 1)].bitcast(FP4X4),
+                                rhs_scale=planes[:, g, first_row + BANK * j : first_row + BANK * (j + 1)],
+                                start=(g == 0),
+                                stop=(g == PASSES - 1),
+                            )
 
-            pooled = keep.tile([P, rows // P, WINDOWS], F32, name="pooled%d" % first_row)
+            by_pixel = [drain.tile([P, BANK], F32, name="by_pixel%d" % j, tag="by_pixel") for j in range(banks)]
             for j in range(banks):
-                by_pixel = drain.tile([P, BANK], F32)
-                nc.scalar.copy(out=by_pixel[:], in_=sums[j][:])
-                by_row = psum.tile([P, BANK], F32, tag="bank")
+                if j % 2 == 0:
+                    nc.scalar.copy(out=by_pixel[j][:], in_=sums[j][:])
+                else:
+                    nc.vector.tensor_copy(out=by_pixel[j][:], in_=sums[j][:])
+            by_row = [psum.tile([P, BANK], F32, name="by_row%d" % j, tag="bank") for j in range(banks)]
+            for j in range(banks):
                 for m in range(BLOCKS):
                     block = slice(P * m, P * (m + 1))
-                    nc.tensor.transpose(by_row[:, block], by_pixel[:, block], by_window[:])
+                    nc.tensor.transpose(by_row[j][:, block], by_pixel[j][:, block], by_window[:])
+            pooled = keep.tile([P, rows // P, WINDOWS], F32, name="pooled%d" % first_row)
+            for j in range(banks):
                 nc.vector.tensor_reduce(
                     out=pooled[:, BLOCKS * j : BLOCKS * (j + 1), :],
-                    in_=by_row[:].rearrange("p (m w d) -> p m w d", m=BLOCKS, d=WINDOW),
+                    in_=by_row[j][:].rearrange("p (m w d) -> p m w d", m=BLOCKS, d=WINDOW),
                     axis=mybir.AxisListType.X,
                     op=mybir.AluOpType.max,
                 )

@@ -26,7 +26,7 @@ PSUM_BANKS = 8
 BLOCKS = BANK // P
 
 QUANT_PASSES = 4
-SCALE_DMA_BYTES = 16384
+SCALE_DMA_BYTES = 32768
 WORD_BUFS = 10
 
 FLOPS = 2 * OUT_ROWS * CHANNELS * PIXELS
@@ -54,7 +54,7 @@ def quantise_image(nc, keep, imgs, img_codes, img_scales):
 
 
 def load_scale_rows(nc, planes, scales_i32, first_pass, stretch, first_row, rows):
-    passes_per_dma = SCALE_DMA_BYTES // rows
+    passes_per_dma = min(stretch, SCALE_DMA_BYTES // rows)
     for g in range(first_pass, first_pass + stretch, passes_per_dma):
         some = slice(g, g + passes_per_dma)
         for q in range(8):

@@ -26,7 +26,7 @@ PSUM_BANKS = 8
 BLOCKS = BANK // P
 
 QUANT_PASSES = 4
-SCALE_DMA_BYTES = 32768
+SCALE_DMA_PASSES = 4
 WORD_BUFS = 10
 
 FLOPS = 2 * OUT_ROWS * CHANNELS * PIXELS
@@ -53,16 +53,13 @@ def quantise_image(nc, keep, imgs, img_codes, img_scales):
         )
 
 
-def load_scale_rows(nc, planes, scales_i32, first_pass, stretch, first_row, rows):
-    passes_per_dma = min(stretch, SCALE_DMA_BYTES // rows)
-    for g in range(first_pass, first_pass + stretch, passes_per_dma):
-        some = slice(g, g + passes_per_dma)
+def load_scale_rows(nc, planes, scales_i32):
+    for g in range(0, PASSES, SCALE_DMA_PASSES):
+        some = slice(g, g + SCALE_DMA_PASSES)
         for q in range(8):
             nc.sync.dma_start(
-                out=planes[32 * (q // 4) + q % 4 : P : 64, some, first_row : first_row + rows].bitcast(I32),
-                in_=scales_i32[some, q : 16 : 8, first_row // 4 : (first_row + rows) // 4].rearrange(
-                    "g q n -> q g n"
-                ),
+                out=planes[32 * (q // 4) + q % 4 : P : 64, some, :].bitcast(I32),
+                in_=scales_i32[some, q : 16 : 8, :].rearrange("g q n -> q g n"),
             )
 
 
@@ -79,13 +76,13 @@ def tile_selfattentionconv2d_pa_k_kernel(tc, imgs, w_kv_words, w_kv_scales, out_
         psum = ctx.enter_context(tc.psum_pool(name="psum", bufs=PSUM_BANKS))
 
         planes = keep.tile([P, PASSES, OUT_ROWS], U8, align_bytes=64)
-        nc.vector.memset(planes[:, 0 : PASSES // 2, :].bitcast(I32), 0)
+        for g in range(0, PASSES, SCALE_DMA_PASSES):
+            nc.vector.memset(planes[:, g : g + SCALE_DMA_PASSES, :].bitcast(I32), 0)
 
         img_codes = keep.tile([P, PASSES * PIXELS], U32, align_bytes=64)
         img_scales = keep.tile([P, PASSES * PIXELS], U8, align_bytes=64)
         quantise_image(nc, keep, imgs[0], img_codes, img_scales)
-
-        nc.vector.memset(planes[:, PASSES // 2 : PASSES, :].bitcast(I32), 0)
+        load_scale_rows(nc, planes, scales_i32)
 
         identity = keep.tile([P, P], F32)
         make_identity(nc, identity[:])
@@ -95,31 +92,29 @@ def tile_selfattentionconv2d_pa_k_kernel(tc, imgs, w_kv_words, w_kv_scales, out_
             in_=identity[:].rearrange("p (i a j b) -> p i j a b", i=8, a=2, j=4, b=2),
         )
 
-        rounds = ((KEY_ROWS, VALUE_ROWS, PASSES // 2, 1, out_1), (0, KEY_ROWS, PASSES, 2, out_0))
-        for first_row, rows, stretch, passes_per_load, out in rounds:
+        rounds = ((KEY_ROWS, VALUE_ROWS, 1, out_1), (0, KEY_ROWS, 2, out_0))
+        for first_row, rows, passes_per_load, out in rounds:
             banks = rows // BANK
             sums = [psum.tile([P, BANK], F32, name="sums%d" % j, tag="bank") for j in range(banks)]
-            for first_pass in range(0, PASSES, stretch):
-                load_scale_rows(nc, planes, scales_i32, first_pass, stretch, first_row, rows)
-                for g0 in range(first_pass, first_pass + stretch, passes_per_load):
-                    words = stream.tile([P, passes_per_load, 2 * rows], U8, align_bytes=64, tag="words")
-                    nc.sync.dma_start(
-                        out=words[:].bitcast(I32),
-                        in_=words_i32[g0 : g0 + passes_per_load, :, first_row // 2 : (first_row + rows) // 2].rearrange(
-                            "g p n -> p g n"
-                        ),
-                    )
-                    for g in range(g0, g0 + passes_per_load):
-                        for j in range(banks):
-                            nc.tensor.matmul_mx(
-                                out=sums[j][:],
-                                lhsT=img_codes[:, g * PIXELS : (g + 1) * PIXELS].bitcast(FP8X4),
-                                lhsT_scale=img_scales[:, g * PIXELS : (g + 1) * PIXELS],
-                                rhs=words[:, g - g0, 2 * BANK * j : 2 * BANK * (j + 1)].bitcast(FP4X4),
-                                rhs_scale=planes[:, g, first_row + BANK * j : first_row + BANK * (j + 1)],
-                                start=(g == 0),
-                                stop=(g == PASSES - 1),
-                            )
+            for g0 in range(0, PASSES, passes_per_load):
+                words = stream.tile([P, passes_per_load, 2 * rows], U8, align_bytes=64, tag="words")
+                nc.sync.dma_start(
+                    out=words[:].bitcast(I32),
+                    in_=words_i32[g0 : g0 + passes_per_load, :, first_row // 2 : (first_row + rows) // 2].rearrange(
+                        "g p n -> p g n"
+                    ),
+                )
+                for g in range(g0, g0 + passes_per_load):
+                    for j in range(banks):
+                        nc.tensor.matmul_mx(
+                            out=sums[j][:],
+                            lhsT=img_codes[:, g * PIXELS : (g + 1) * PIXELS].bitcast(FP8X4),
+                            lhsT_scale=img_scales[:, g * PIXELS : (g + 1) * PIXELS],
+                            rhs=words[:, g - g0, 2 * BANK * j : 2 * BANK * (j + 1)].bitcast(FP4X4),
+                            rhs_scale=planes[:, g, first_row + BANK * j : first_row + BANK * (j + 1)],
+                            start=(g == 0),
+                            stop=(g == PASSES - 1),
+                        )
 
             by_pixel = [drain.tile([P, BANK], F32, name="by_pixel%d" % j, tag="by_pixel") for j in range(banks)]
             for j in range(banks):

@@ -26,7 +26,7 @@ PSUM_BANKS = 8
 BLOCKS = BANK // P
 
 QUANT_PASSES = 4
-SCALE_DMA_PASSES = 4
+SCALE_DMA_PASSES = (4, 4, 4, 3, 1)
 WORD_BUFS = 10
 
 FLOPS = 2 * OUT_ROWS * CHANNELS * PIXELS
@@ -54,8 +54,10 @@ def quantise_image(nc, keep, imgs, img_codes, img_scales):
 
 
 def load_scale_rows(nc, planes, scales_i32):
-    for g in range(0, PASSES, SCALE_DMA_PASSES):
-        some = slice(g, g + SCALE_DMA_PASSES)
+    g = 0
+    for passes in SCALE_DMA_PASSES:
+        some = slice(g, g + passes)
+        g += passes
         for q in range(8):
             nc.sync.dma_start(
                 out=planes[32 * (q // 4) + q % 4 : P : 64, some, :].bitcast(I32),
@@ -76,8 +78,10 @@ def tile_selfattentionconv2d_pa_k_kernel(tc, imgs, w_kv_words, w_kv_scales, out_
         psum = ctx.enter_context(tc.psum_pool(name="psum", bufs=PSUM_BANKS))
 
         planes = keep.tile([P, PASSES, OUT_ROWS], U8, align_bytes=64)
-        for g in range(0, PASSES, SCALE_DMA_PASSES):
-            nc.vector.memset(planes[:, g : g + SCALE_DMA_PASSES, :].bitcast(I32), 0)
+        g = 0
+        for passes in SCALE_DMA_PASSES:
+            nc.vector.memset(planes[:, g : g + passes, :].bitcast(I32), 0)
+            g += passes
 
         img_codes = keep.tile([P, PASSES * PIXELS], U32, align_bytes=64)
         img_scales = keep.tile([P, PASSES * PIXELS], U8, align_bytes=64)

@@ -27,6 +27,11 @@ BLOCKS = BANK // P
 
 QUANT_PASSES = 4
 SCALE_DMA_PASSES = (4, 4, 4, 3, 1)
+BANKS = OUT_ROWS // BANK
+KEY_BANKS = KEY_ROWS // BANK
+FIRST_BANKS = 6
+LAST_PASSES = 2
+TRANSPOSE_BANK = (2, 3, 4, 5)
 WORD_BUFS = 10
 
 FLOPS = 2 * OUT_ROWS * CHANNELS * PIXELS
@@ -75,7 +80,7 @@ def tile_selfattentionconv2d_pa_k_kernel(tc, imgs, w_kv_words, w_kv_scales, out_
         keep = ctx.enter_context(tc.tile_pool(name="keep", bufs=1))
         stream = ctx.enter_context(tc.tile_pool(name="stream", bufs=WORD_BUFS))
         drain = ctx.enter_context(tc.tile_pool(name="drain", bufs=PSUM_BANKS))
-        psum = ctx.enter_context(tc.psum_pool(name="psum", bufs=PSUM_BANKS))
+        psum = ctx.enter_context(tc.psum_pool(name="psum", bufs=1))
 
         planes = keep.tile([P, PASSES, OUT_ROWS], U8, align_bytes=64)
         g = 0
@@ -96,47 +101,88 @@ def tile_selfattentionconv2d_pa_k_kernel(tc, imgs, w_kv_words, w_kv_scales, out_
             in_=identity[:].rearrange("p (i a j b) -> p i j a b", i=8, a=2, j=4, b=2),
         )
 
-        rounds = ((KEY_ROWS, VALUE_ROWS, 1, out_1), (0, KEY_ROWS, 2, out_0))
-        for first_row, rows, passes_per_load, out in rounds:
-            banks = rows // BANK
-            sums = [psum.tile([P, BANK], F32, name="sums%d" % j, tag="bank") for j in range(banks)]
-            for g0 in range(0, PASSES, passes_per_load):
-                words = stream.tile([P, passes_per_load, 2 * rows], U8, align_bytes=64, tag="words")
-                nc.sync.dma_start(
-                    out=words[:].bitcast(I32),
-                    in_=words_i32[g0 : g0 + passes_per_load, :, first_row // 2 : (first_row + rows) // 2].rearrange(
-                        "g p n -> p g n"
-                    ),
-                )
-                for g in range(g0, g0 + passes_per_load):
-                    for j in range(banks):
-                        nc.tensor.matmul_mx(
-                            out=sums[j][:],
-                            lhsT=img_codes[:, g * PIXELS : (g + 1) * PIXELS].bitcast(FP8X4),
-                            lhsT_scale=img_scales[:, g * PIXELS : (g + 1) * PIXELS],
-                            rhs=words[:, g - g0, 2 * BANK * j : 2 * BANK * (j + 1)].bitcast(FP4X4),
-                            rhs_scale=planes[:, g, first_row + BANK * j : first_row + BANK * (j + 1)],
-                            start=(g == 0),
-                            stop=(g == PASSES - 1),
-                        )
+        pooled = keep.tile([P, OUT_ROWS // P, WINDOWS], F32)
+        by_pixel = {}
 
-            by_pixel = [drain.tile([P, BANK], F32, name="by_pixel%d" % j, tag="by_pixel") for j in range(banks)]
-            for j in range(banks):
-                if j % 2 == 0:
-                    nc.scalar.copy(out=by_pixel[j][:], in_=sums[j][:])
-                else:
-                    nc.vector.tensor_copy(out=by_pixel[j][:], in_=sums[j][:])
-            by_row = [psum.tile([P, BANK], F32, name="by_row%d" % j, tag="bank") for j in range(banks)]
-            for j in range(banks):
-                for m in range(BLOCKS):
-                    block = slice(P * m, P * (m + 1))
-                    nc.tensor.transpose(by_row[j][:, block], by_pixel[j][:, block], by_window[:])
-            pooled = keep.tile([P, rows // P, WINDOWS], F32, name="pooled%d" % first_row)
-            for j in range(banks):
-                nc.vector.tensor_reduce(
-                    out=pooled[:, BLOCKS * j : BLOCKS * (j + 1), :],
-                    in_=by_row[j][:].rearrange("p (m w d) -> p m w d", m=BLOCKS, d=WINDOW),
-                    axis=mybir.AxisListType.X,
-                    op=mybir.AluOpType.max,
-                )
-            nc.scalar.dma_start(out=out[0].rearrange("(m p) i j -> p m (i j)", p=P), in_=pooled[:])
+        def load_words(first_bank, banks, g0, passes):
+            words = stream.tile([P, passes, 2 * BANK * banks], U8, align_bytes=64, tag="words")
+            some = slice(first_bank * BANK // 2, (first_bank + banks) * BANK // 2)
+            nc.sync.dma_start(
+                out=words[:].bitcast(I32),
+                in_=words_i32[g0 : g0 + passes, :, some].rearrange("g p n -> p g n"),
+            )
+            return words
+
+        def multiply(total, words, g, slot, j, word_bank):
+            nc.tensor.matmul_mx(
+                out=total[:],
+                lhsT=img_codes[:, g * PIXELS : (g + 1) * PIXELS].bitcast(FP8X4),
+                lhsT_scale=img_scales[:, g * PIXELS : (g + 1) * PIXELS],
+                rhs=words[:, slot, 2 * BANK * word_bank : 2 * BANK * (word_bank + 1)].bitcast(FP4X4),
+                rhs_scale=planes[:, g, BANK * j : BANK * (j + 1)],
+                start=(g == 0),
+                stop=(g == PASSES - 1),
+            )
+
+        def empty(total, j):
+            by_pixel[j] = drain.tile([P, BANK], F32, name="by_pixel%d" % j, tag="by_pixel")
+            grouped_rows = by_pixel[j][:].rearrange("x (m p) -> x m p", m=BLOCKS)
+            bank_rows = total[:].rearrange("x (p m) -> x m p", m=BLOCKS)
+            if j % 2 == 0:
+                nc.scalar.copy(out=grouped_rows, in_=bank_rows)
+            else:
+                nc.vector.tensor_copy(out=grouped_rows, in_=bank_rows)
+
+        def pool(j):
+            by_row = psum.tile([P, BANK], F32, name="by_row%d" % j, tag="bank%d" % TRANSPOSE_BANK[j % 4])
+            for m in range(BLOCKS):
+                block = slice(P * m, P * (m + 1))
+                nc.tensor.transpose(by_row[:, block], by_pixel[j][:, block], by_window[:])
+            nc.vector.tensor_reduce(
+                out=pooled[:, BLOCKS * j : BLOCKS * (j + 1), :],
+                in_=by_row[:].rearrange("p (m w d) -> p m w d", m=BLOCKS, d=WINDOW),
+                axis=mybir.AxisListType.X,
+                op=mybir.AluOpType.max,
+            )
+
+        totals = [psum.tile([P, BANK], F32, name="total%d" % j, tag="bank%d" % j) for j in range(FIRST_BANKS)]
+        for g in range(PASSES):
+            words = load_words(0, FIRST_BANKS, g, 1)
+            for j in range(FIRST_BANKS):
+                multiply(totals[j], words, g, 0, j, j)
+        for j in range(FIRST_BANKS):
+            empty(totals[j], j)
+
+        last_banks = range(FIRST_BANKS, BANKS)
+        totals = {
+            j: psum.tile([P, BANK], F32, name="total%d" % j, tag="bank%d" % (j % PSUM_BANKS)) for j in last_banks
+        }
+        for g0 in range(0, PASSES - LAST_PASSES, LAST_PASSES):
+            words = load_words(FIRST_BANKS, BANKS - FIRST_BANKS, g0, LAST_PASSES)
+            for g in range(g0, g0 + LAST_PASSES):
+                for j in last_banks:
+                    multiply(totals[j], words, g, g - g0, j, j - FIRST_BANKS)
+                if 1 <= g <= FIRST_BANKS:
+                    pool(g - 1)
+        g0 = PASSES - LAST_PASSES
+        words = load_words(FIRST_BANKS, BANKS - FIRST_BANKS, g0, LAST_PASSES)
+        for j in last_banks:
+            for g in range(g0, PASSES):
+                multiply(totals[j], words, g, g - g0, j, j - FIRST_BANKS)
+            empty(totals[j], j)
+            if j - 2 in last_banks:
+                pool(j - 2)
+        for j in last_banks[-2:]:
+            pool(j)
+
+        for out, first_bank, end_bank, row in (
+            (out_0, 0, KEY_BANKS, 0),
+            (out_1, KEY_BANKS, FIRST_BANKS, 0),
+            (out_1, FIRST_BANKS, BANKS - 2, FIRST_BANKS - KEY_BANKS),
+            (out_1, BANKS - 2, BANKS, BANKS - 2 - KEY_BANKS),
+        ):
+            some = slice(BANK * row, BANK * (row + end_bank - first_bank))
+            nc.sync.dma_start(
+                out=out[0, some].rearrange("(j p m) y x -> p j (m y x)", p=P, m=BLOCKS),
+                in_=pooled[:, BLOCKS * first_bank : BLOCKS * end_bank, :].rearrange("p (j m) w -> p j (m w)", m=BLOCKS),
+            )

@@ -26,10 +26,11 @@ PSUM_BANKS = 8
 BLOCKS = BANK // P
 
 QUANT_PASSES = 4
-SCALE_DMA_PASSES = (4, 4, 4, 3, 1)
+SCALE_DMA_PASSES = (4, 4, 4, 2, 2)
 BANKS = OUT_ROWS // BANK
 KEY_BANKS = KEY_ROWS // BANK
 FIRST_BANKS = 6
+LOAD_PASSES = 2
 LAST_PASSES = 2
 TRANSPOSE_BANK = (2, 3, 4, 5)
 WORD_BUFS = 10
@@ -79,7 +80,8 @@ def tile_selfattentionconv2d_pa_k_kernel(tc, imgs, w_kv_words, w_kv_scales, out_
         ctx.enter_context(tc.manual_schedule())
         keep = ctx.enter_context(tc.tile_pool(name="keep", bufs=1))
         stream = ctx.enter_context(tc.tile_pool(name="stream", bufs=WORD_BUFS))
-        drain = ctx.enter_context(tc.tile_pool(name="drain", bufs=PSUM_BANKS))
+        drain = ctx.enter_context(tc.tile_pool(name="drain", bufs=BANKS - FIRST_BANKS))
+        turned = ctx.enter_context(tc.tile_pool(name="turned", bufs=FIRST_BANKS))
         psum = ctx.enter_context(tc.psum_pool(name="psum", bufs=1))
 
         planes = keep.tile([P, PASSES, OUT_ROWS], U8, align_bytes=64)
@@ -101,8 +103,12 @@ def tile_selfattentionconv2d_pa_k_kernel(tc, imgs, w_kv_words, w_kv_scales, out_
             in_=identity[:].rearrange("p (i a j b) -> p i j a b", i=8, a=2, j=4, b=2),
         )
 
-        pooled = keep.tile([P, OUT_ROWS // P, WINDOWS], F32)
+        first_pooled = keep.tile([P, BLOCKS * FIRST_BANKS, WINDOWS], F32)
+        last_pooled = keep.tile([P, BLOCKS * (BANKS - FIRST_BANKS), WINDOWS], F32)
         by_pixel = {}
+        by_quadrant = {}
+        window_rows = {}
+        in_order = {}
 
         def load_words(first_bank, banks, g0, passes):
             words = stream.tile([P, passes, 2 * BANK * banks], U8, align_bytes=64, tag="words")
@@ -133,13 +139,41 @@ def tile_selfattentionconv2d_pa_k_kernel(tc, imgs, w_kv_words, w_kv_scales, out_
             else:
                 nc.vector.tensor_copy(out=grouped_rows, in_=bank_rows)
 
+        def turn(total, j):
+            by_quadrant[j] = turned.tile([P, BANK], F32, name="by_quadrant%d" % j, align_bytes=64, tag="by_quadrant")
+            nc.vector.transpose(by_quadrant[j][:], total[:])
+
+        def pool_quadrants(j):
+            window_rows[j] = turned.tile([P, P], F32, name="window_rows%d" % j, align_bytes=64, tag="window_rows")
+            nc.vector.tensor_reduce(
+                out=window_rows[j][:].rearrange("p (sy x) -> p sy x", x=4),
+                in_=by_quadrant[j][:].rearrange("p (sy a x b) -> p sy x a b", a=2, x=4, b=2),
+                axis=mybir.AxisListType.XY,
+                op=mybir.AluOpType.max,
+            )
+            in_order[j] = turned.tile([P, P], F32, name="in_order%d" % j, tag="in_order")
+            nc.scalar.copy(
+                out=in_order[j][:].rearrange("p (c m w) -> p c m w", c=4, m=BLOCKS),
+                in_=window_rows[j][:].rearrange("p (m c w) -> p c m w", c=4, m=BLOCKS),
+            )
+
+        def gather(j):
+            swapped = psum.tile([P, P], F32, name="swapped%d" % j, tag="bank%d" % TRANSPOSE_BANK[j % 4])
+            nc.tensor.transpose(swapped[:], in_order[j][:], identity[:])
+            gathered = turned.tile([P, P], F32, name="gathered%d" % j, align_bytes=64, tag="gathered")
+            nc.vector.transpose(gathered[:], swapped[:])
+            nc.scalar.copy(
+                out=first_pooled[:, BLOCKS * j : BLOCKS * (j + 1), :].rearrange("p m (k w) -> p m k w", k=4),
+                in_=gathered[:].rearrange("p (k m w) -> p m k w", k=4, m=BLOCKS),
+            )
+
         def pool(j):
             by_row = psum.tile([P, BANK], F32, name="by_row%d" % j, tag="bank%d" % TRANSPOSE_BANK[j % 4])
             for m in range(BLOCKS):
                 block = slice(P * m, P * (m + 1))
                 nc.tensor.transpose(by_row[:, block], by_pixel[j][:, block], by_window[:])
             nc.vector.tensor_reduce(
-                out=pooled[:, BLOCKS * j : BLOCKS * (j + 1), :],
+                out=last_pooled[:, BLOCKS * (j - FIRST_BANKS) : BLOCKS * (j - FIRST_BANKS + 1), :],
                 in_=by_row[:].rearrange("p (m w d) -> p m w d", m=BLOCKS, d=WINDOW),
                 axis=mybir.AxisListType.X,
                 op=mybir.AluOpType.max,
@@ -150,39 +184,44 @@ def tile_selfattentionconv2d_pa_k_kernel(tc, imgs, w_kv_words, w_kv_scales, out_
             words = load_words(0, FIRST_BANKS, g, 1)
             for j in range(FIRST_BANKS):
                 multiply(totals[j], words, g, 0, j, j)
-        for j in range(FIRST_BANKS):
-            empty(totals[j], j)
+        turn(totals[0], 0)
+        for j in range(1, FIRST_BANKS):
+            turn(totals[j], j)
+            pool_quadrants(j - 1)
+        pool_quadrants(FIRST_BANKS - 1)
 
         last_banks = range(FIRST_BANKS, BANKS)
         totals = {
             j: psum.tile([P, BANK], F32, name="total%d" % j, tag="bank%d" % (j % PSUM_BANKS)) for j in last_banks
         }
-        for g0 in range(0, PASSES - LAST_PASSES, LAST_PASSES):
-            words = load_words(FIRST_BANKS, BANKS - FIRST_BANKS, g0, LAST_PASSES)
-            for g in range(g0, g0 + LAST_PASSES):
-                for j in last_banks:
+        for g0 in range(0, PASSES - LAST_PASSES, LOAD_PASSES):
+            words = load_words(FIRST_BANKS, BANKS - FIRST_BANKS, g0, LOAD_PASSES)
+            for j in last_banks:
+                for g in range(g0, g0 + LOAD_PASSES):
                     multiply(totals[j], words, g, g - g0, j, j - FIRST_BANKS)
-                if 1 <= g <= FIRST_BANKS:
-                    pool(g - 1)
-        g0 = PASSES - LAST_PASSES
-        words = load_words(FIRST_BANKS, BANKS - FIRST_BANKS, g0, LAST_PASSES)
+            if g0 >= LOAD_PASSES:
+                gather(g0 // LOAD_PASSES - 1)
+        last_words = {
+            g: load_words(FIRST_BANKS, BANKS - FIRST_BANKS, g, 1) for g in range(PASSES - LAST_PASSES, PASSES)
+        }
         for j in last_banks:
-            for g in range(g0, PASSES):
-                multiply(totals[j], words, g, g - g0, j, j - FIRST_BANKS)
+            for g, words in last_words.items():
+                multiply(totals[j], words, g, 0, j, j - FIRST_BANKS)
             empty(totals[j], j)
             if j - 2 in last_banks:
                 pool(j - 2)
         for j in last_banks[-2:]:
             pool(j)
 
-        for out, first_bank, end_bank, row in (
-            (out_0, 0, KEY_BANKS, 0),
-            (out_1, KEY_BANKS, FIRST_BANKS, 0),
-            (out_1, FIRST_BANKS, BANKS - 2, FIRST_BANKS - KEY_BANKS),
-            (out_1, BANKS - 2, BANKS, BANKS - 2 - KEY_BANKS),
-        ):
-            some = slice(BANK * row, BANK * (row + end_bank - first_bank))
+        for out, first_bank, end_bank in ((out_0, 0, KEY_BANKS), (out_1, KEY_BANKS, FIRST_BANKS)):
             nc.sync.dma_start(
-                out=out[0, some].rearrange("(j p m) y x -> p j (m y x)", p=P, m=BLOCKS),
-                in_=pooled[:, BLOCKS * first_bank : BLOCKS * end_bank, :].rearrange("p (j m) w -> p j (m w)", m=BLOCKS),
+                out=out[0, 0 : BANK * (end_bank - first_bank)].rearrange("(m p) y x -> p m (y x)", p=P),
+                in_=first_pooled[:, BLOCKS * first_bank : BLOCKS * end_bank, :],
+            )
+        for first_bank, end_bank in ((FIRST_BANKS, BANKS - 1), (BANKS - 1, BANKS)):
+            some = slice(BANK * (first_bank - KEY_BANKS), BANK * (end_bank - KEY_BANKS))
+            columns = slice(BLOCKS * (first_bank - FIRST_BANKS), BLOCKS * (end_bank - FIRST_BANKS))
+            nc.scalar.dma_start(
+                out=out_1[0, some].rearrange("(j p m) y x -> p j (m y x)", p=P, m=BLOCKS),
+                in_=last_pooled[:, columns, :].rearrange("p (j m) w -> p j (m w)", m=BLOCKS),
             )

from contextlib import ExitStack

import concourse.mybir as mybir
from concourse.masks import make_identity

F32 = mybir.dt.float32
BF16 = mybir.dt.bfloat16
I32 = mybir.dt.int32
U32 = mybir.dt.uint32
U8 = mybir.dt.uint8
FP8X4 = mybir.dt.float8_e4m3fn_x4
FP4X4 = mybir.dt.float4_e2m1fn_x4

P = 128
PACK = 4
CHANNELS = 8192
PASSES = CHANNELS // (P * PACK)
PIXELS = 128
WINDOWS = 32
WINDOW = 4
KEY_ROWS = 1024
VALUE_ROWS = 4096
OUT_ROWS = KEY_ROWS + VALUE_ROWS
BANK = 512
PSUM_BANKS = 8
BLOCKS = BANK // P

QUANT_PASSES = 4
SCALE_DMA_PASSES = (4, 4, 4, 2, 2)
BANKS = OUT_ROWS // BANK
KEY_BANKS = KEY_ROWS // BANK
FIRST_BANKS = 6
LOAD_PASSES = 2
LAST_PASSES = 2
TRANSPOSE_BANK = (2, 3, 4, 5)
WORD_BUFS = 10

FLOPS = 2 * OUT_ROWS * CHANNELS * PIXELS


def quantise_image(nc, keep, imgs, img_codes, img_scales):
    raw = keep.tile([P, PASSES, PACK, PIXELS], BF16)
    grouped = keep.tile([P, PASSES, PIXELS, PACK], BF16, align_bytes=64)
    by_pass = imgs.rearrange("(g p t) h w -> p g t (h w)", p=P, t=PACK)
    chunk_starts = range(0, PASSES, QUANT_PASSES)
    for g in chunk_starts:
        nc.sync.dma_start(out=raw[:, g : g + QUANT_PASSES], in_=by_pass[:, g : g + QUANT_PASSES])
    for g in chunk_starts:
        nc.vector.tensor_copy(
            out=grouped[:, g : g + QUANT_PASSES],
            in_=raw[:, g : g + QUANT_PASSES].rearrange("p g t x -> p g x t"),
        )
    for g in chunk_starts:
        columns = slice(g * PIXELS, (g + QUANT_PASSES) * PIXELS)
        nc.vector.quantize_mx(
            out=img_codes[:, columns].bitcast(FP8X4),
            scales=img_scales[:, columns],
            in_=grouped[:, g : g + QUANT_PASSES].rearrange("p g x t -> p (g x t)"),
        )


def load_scale_rows(nc, planes, scales_i32):
    g = 0
    for passes in SCALE_DMA_PASSES:
        some = slice(g, g + passes)
        g += passes
        for q in range(8):
            nc.sync.dma_start(
                out=planes[32 * (q // 4) + q % 4 : P : 64, some, :].bitcast(I32),
                in_=scales_i32[some, q : 16 : 8, :].rearrange("g q n -> q g n"),
            )


def tile_selfattentionconv2d_pa_k_kernel(tc, imgs, w_kv_words, w_kv_scales, out_0, out_1):
    nc = tc.nc
    words_i32 = w_kv_words.bitcast(I32)
    scales_i32 = w_kv_scales.bitcast(I32)

    with ExitStack() as ctx:
        ctx.enter_context(tc.manual_schedule())
        keep = ctx.enter_context(tc.tile_pool(name="keep", bufs=1))
        stream = ctx.enter_context(tc.tile_pool(name="stream", bufs=WORD_BUFS))
        drain = ctx.enter_context(tc.tile_pool(name="drain", bufs=BANKS - FIRST_BANKS))
        turned = ctx.enter_context(tc.tile_pool(name="turned", bufs=FIRST_BANKS))
        psum = ctx.enter_context(tc.psum_pool(name="psum", bufs=1))

        planes = keep.tile([P, PASSES, OUT_ROWS], U8, align_bytes=64)
        g = 0
        for passes in SCALE_DMA_PASSES:
            nc.vector.memset(planes[:, g : g + passes, :].bitcast(I32), 0)
            g += passes

        img_codes = keep.tile([P, PASSES * PIXELS], U32, align_bytes=64)
        img_scales = keep.tile([P, PASSES * PIXELS], U8, align_bytes=64)
        quantise_image(nc, keep, imgs[0], img_codes, img_scales)
        load_scale_rows(nc, planes, scales_i32)

        identity = keep.tile([P, P], F32)
        make_identity(nc, identity[:])
        by_window = keep.tile([P, P], F32)
        nc.vector.tensor_copy(
            out=by_window[:].rearrange("p (i j a b) -> p i j a b", i=8, j=4, a=2, b=2),
            in_=identity[:].rearrange("p (i a j b) -> p i j a b", i=8, a=2, j=4, b=2),
        )

        first_pooled = keep.tile([P, BLOCKS * FIRST_BANKS, WINDOWS], F32)
        last_pooled = keep.tile([P, BLOCKS * (BANKS - FIRST_BANKS), WINDOWS], F32)
        by_pixel = {}
        by_quadrant = {}
        window_rows = {}
        in_order = {}

        def load_words(first_bank, banks, g0, passes):
            words = stream.tile([P, passes, 2 * BANK * banks], U8, align_bytes=64, tag="words")
            some = slice(first_bank * BANK // 2, (first_bank + banks) * BANK // 2)
            nc.sync.dma_start(
                out=words[:].bitcast(I32),
                in_=words_i32[g0 : g0 + passes, :, some].rearrange("g p n -> p g n"),
            )
            return words

        def multiply(total, words, g, slot, j, word_bank):
            nc.tensor.matmul_mx(
                out=total[:],
                lhsT=img_codes[:, g * PIXELS : (g + 1) * PIXELS].bitcast(FP8X4),
                lhsT_scale=img_scales[:, g * PIXELS : (g + 1) * PIXELS],
                rhs=words[:, slot, 2 * BANK * word_bank : 2 * BANK * (word_bank + 1)].bitcast(FP4X4),
                rhs_scale=planes[:, g, BANK * j : BANK * (j + 1)],
                start=(g == 0),
                stop=(g == PASSES - 1),
            )

        def empty(total, j):
            by_pixel[j] = drain.tile([P, BANK], F32, name="by_pixel%d" % j, tag="by_pixel")
            grouped_rows = by_pixel[j][:].rearrange("x (m p) -> x m p", m=BLOCKS)
            bank_rows = total[:].rearrange("x (p m) -> x m p", m=BLOCKS)
            if j % 2 == 0:
                nc.scalar.copy(out=grouped_rows, in_=bank_rows)
            else:
                nc.vector.tensor_copy(out=grouped_rows, in_=bank_rows)

        def turn(total, j):
            by_quadrant[j] = turned.tile([P, BANK], F32, name="by_quadrant%d" % j, align_bytes=64, tag="by_quadrant")
            nc.vector.transpose(by_quadrant[j][:], total[:])

        def pool_quadrants(j):
            window_rows[j] = turned.tile([P, P], F32, name="window_rows%d" % j, align_bytes=64, tag="window_rows")
            nc.vector.tensor_reduce(
                out=window_rows[j][:].rearrange("p (sy x) -> p sy x", x=4),
                in_=by_quadrant[j][:].rearrange("p (sy a x b) -> p sy x a b", a=2, x=4, b=2),
                axis=mybir.AxisListType.XY,
                op=mybir.AluOpType.max,
            )
            in_order[j] = turned.tile([P, P], F32, name="in_order%d" % j, tag="in_order")
            nc.scalar.copy(
                out=in_order[j][:].rearrange("p (c m w) -> p c m w", c=4, m=BLOCKS),
                in_=window_rows[j][:].rearrange("p (m c w) -> p c m w", c=4, m=BLOCKS),
            )

        def gather(j):
            swapped = psum.tile([P, P], F32, name="swapped%d" % j, tag="bank%d" % TRANSPOSE_BANK[j % 4])
            nc.tensor.transpose(swapped[:], in_order[j][:], identity[:])
            gathered = turned.tile([P, P], F32, name="gathered%d" % j, align_bytes=64, tag="gathered")
            nc.vector.transpose(gathered[:], swapped[:])
            nc.scalar.copy(
                out=first_pooled[:, BLOCKS * j : BLOCKS * (j + 1), :].rearrange("p m (k w) -> p m k w", k=4),
                in_=gathered[:].rearrange("p (k m w) -> p m k w", k=4, m=BLOCKS),
            )

        def pool(j):
            by_row = psum.tile([P, BANK], F32, name="by_row%d" % j, tag="bank%d" % TRANSPOSE_BANK[j % 4])
            for m in range(BLOCKS):
                block = slice(P * m, P * (m + 1))
                nc.tensor.transpose(by_row[:, block], by_pixel[j][:, block], by_window[:])
            nc.vector.tensor_reduce(
                out=last_pooled[:, BLOCKS * (j - FIRST_BANKS) : BLOCKS * (j - FIRST_BANKS + 1), :],
                in_=by_row[:].rearrange("p (m w d) -> p m w d", m=BLOCKS, d=WINDOW),
                axis=mybir.AxisListType.X,
                op=mybir.AluOpType.max,
            )

        totals = [psum.tile([P, BANK], F32, name="total%d" % j, tag="bank%d" % j) for j in range(FIRST_BANKS)]
        for g in range(PASSES):
            words = load_words(0, FIRST_BANKS, g, 1)
            for j in range(FIRST_BANKS):
                multiply(totals[j], words, g, 0, j, j)
        turn(totals[0], 0)
        for j in range(1, FIRST_BANKS):
            turn(totals[j], j)
            pool_quadrants(j - 1)
        pool_quadrants(FIRST_BANKS - 1)

        last_banks = range(FIRST_BANKS, BANKS)
        totals = {
            j: psum.tile([P, BANK], F32, name="total%d" % j, tag="bank%d" % (j % PSUM_BANKS)) for j in last_banks
        }
        for g0 in range(0, PASSES - LAST_PASSES, LOAD_PASSES):
            words = load_words(FIRST_BANKS, BANKS - FIRST_BANKS, g0, LOAD_PASSES)
            for j in last_banks:
                for g in range(g0, g0 + LOAD_PASSES):
                    multiply(totals[j], words, g, g - g0, j, j - FIRST_BANKS)
            if g0 >= LOAD_PASSES:
                gather(g0 // LOAD_PASSES - 1)
        last_words = {
            g: load_words(FIRST_BANKS, BANKS - FIRST_BANKS, g, 1) for g in range(PASSES - LAST_PASSES, PASSES)
        }
        for j in last_banks:
            for g, words in last_words.items():
                multiply(totals[j], words, g, 0, j, j - FIRST_BANKS)
            empty(totals[j], j)
            if j - 2 in last_banks:
                pool(j - 2)
        for j in last_banks[-2:]:
            pool(j)

        for out, first_bank, end_bank in ((out_0, 0, KEY_BANKS), (out_1, KEY_BANKS, FIRST_BANKS)):
            nc.sync.dma_start(
                out=out[0, 0 : BANK * (end_bank - first_bank)].rearrange("(m p) y x -> p m (y x)", p=P),
                in_=first_pooled[:, BLOCKS * first_bank : BLOCKS * end_bank, :],
            )
        for first_bank, end_bank in ((FIRST_BANKS, BANKS - 1), (BANKS - 1, BANKS)):
            some = slice(BANK * (first_bank - KEY_BANKS), BANK * (end_bank - KEY_BANKS))
            columns = slice(BLOCKS * (first_bank - FIRST_BANKS), BLOCKS * (end_bank - FIRST_BANKS))
            nc.scalar.dma_start(
                out=out_1[0, some].rearrange("(j p m) y x -> p j (m y x)", p=P, m=BLOCKS),
                in_=last_pooled[:, columns, :].rearrange("p (j m) w -> p j (m w)", m=BLOCKS),
            )
